import numpy as np
import ml_dtypes


def mxq(x, axis, fmt="e4m3"):
    dtype, down = {"e4m3": (ml_dtypes.float8_e4m3fn, 7), "e5m2": (ml_dtypes.float8_e5m2, 14)}[fmt]
    v = np.moveaxis(np.asarray(x, np.float32).astype(ml_dtypes.bfloat16).astype(np.float64), axis, -1)
    blocks = v.reshape(v.shape[:-1] + (-1, 32))
    amax = np.abs(blocks).max(-1, keepdims=True)
    byte = np.maximum(np.where(amax > 0, np.frexp(amax)[1] - 1 + 127, 0) - down, 1)
    scale = np.exp2(byte - 127.0)
    codes = (blocks / scale).astype(np.float32).astype(dtype).astype(np.float64)
    return np.moveaxis((codes * scale).reshape(v.shape), -1, axis)


WIDE = False


def mx_kscale(k):
    if not WIDE:
        return np.ones(k)
    levels = np.array([10, -10, 5, -5, 0])
    a = np.random.permutation(np.resize(levels, k // 512 * 4)).reshape(k // 512, 4)
    idx = np.arange(k)
    return np.exp2(a[idx // 512, idx % 128 // 32])


BF16 = ml_dtypes.bfloat16


def bf(x):
    return np.asarray(x, np.float32).astype(BF16)


def f64(x):
    return np.asarray(x).astype(np.float64)


T, B, D, H, L = 32, 128, 1024, 256, 1
G = 4


def sigmoid(v):
    return 1.0 / (1.0 + np.exp(-v))


def setup_inputs():
    s = mx_kscale(D)
    W = np.random.standard_normal((L, G, D + H, H)) * 1.5 / np.sqrt(D + H)
    W[0, :, :D, :] /= s[:, None]
    return {"inputs": bf(np.random.standard_normal((T, B, D)) * s),
            "h_0": bf(np.random.standard_normal((L, B, H)) * 0.5),
            "c_0": bf(np.random.standard_normal((L, B, H))),
            "W": bf(W),
            "b": bf(np.random.standard_normal((L, G, H)) * 0.3)}


def reference(inputs, h_0, c_0, W, b):
    x = f64(inputs)
    h_0, c_0, W, b = f64(h_0), f64(c_0), f64(W), f64(b)
    h_layers, c_layers = [], []
    for l in range(L):
        wx = W[l][:, :D, :].transpose(1, 0, 2).reshape(D, G * H)
        wh = W[l][:, D:, :].transpose(1, 0, 2).reshape(H, G * H)
        xin = x if l == 0 else x
        gx = (mxq(xin.reshape(T * B, D), 1, "e4m3") @ mxq(wx, 0, "e4m3")).reshape(T, B, G, H)
        gh = (h_0[l] @ wh).reshape(B, G, H)
        gates = gx + gh + b[l]
        f = sigmoid(gates[..., 0, :])
        i = sigmoid(gates[..., 1, :])
        g = np.tanh(gates[..., 2, :])
        o = sigmoid(gates[..., 3, :])
        c = f * c_0[l] + i * g
        h = o * np.tanh(c)
        x = h
        h_layers.append(h)
        c_layers.append(c)
    h_n = np.stack(h_layers, axis=1)
    c_n = np.stack(c_layers, axis=1)
    return x, np.stack([h_n, c_n], axis=0)

@@ -1,0 +1,264 @@
+from contextlib import ExitStack
+
+import concourse.mybir as mybir
+from concourse.masks import make_identity
+
+F32 = mybir.dt.float32
+BF16 = mybir.dt.bfloat16
+U32 = mybir.dt.uint32
+U8 = mybir.dt.uint8
+FP8X4 = mybir.dt.float8_e4m3fn_x4
+SIGMOID = mybir.ActivationFunctionType.Sigmoid
+TANH = mybir.ActivationFunctionType.Tanh
+ADD = mybir.AluOpType.add
+MULT = mybir.AluOpType.mult
+
+T, B, D, H, GATES = 32, 128, 1024, 256, 4
+P = 128
+PACK = 4
+K_PASS = P * PACK
+PASSES = D // K_PASS
+GATE_COLS = GATES * H
+BANK = 512
+HALVES = GATE_COLS // BANK
+GATES_PER_HALF = GATES // HALVES
+SUBS = 2
+ROUND_ROWS = SUBS * P
+ROUNDS = T * B // ROUND_ROWS
+WORDS = D // 2
+X_BUFS = 6
+
+FLOPS = 2 * T * B * D * GATE_COLS + 2 * B * H * GATE_COLS
+
+
+def tile_qlstm_t_kernel(tc, inputs, h_0, c_0, W, b, out_0, out_1):
+    nc = tc.nc
+    x_rows = inputs.flatten_outer_dims()
+    h_rows = out_0.flatten_outer_dims()
+    hc_rows = out_1.rearrange("a t l n h -> a (t l n) h")
+
+    with ExitStack() as stack:
+        const = stack.enter_context(tc.tile_pool(name="const", bufs=1))
+        x_pool = stack.enter_context(tc.tile_pool(name="x_pool", bufs=X_BUFS))
+        work = stack.enter_context(tc.tile_pool(name="work", bufs=3))
+        late = stack.enter_context(tc.tile_pool(name="late", bufs=4))
+        psum_t = stack.enter_context(tc.psum_pool(name="psum_t", bufs=2))
+        psum_g = stack.enter_context(tc.psum_pool(name="psum_g", bufs=6))
+
+        ident = const.tile([P, P], F32)
+        ones = const.tile([P, P], BF16)
+        b_row = const.tile([P, GATE_COLS], BF16)
+        w_raw = const.tile([P, PASSES * GATES, PACK * H], BF16)
+        w_grouped = const.tile([P, PASSES * GATES, H * PACK], BF16, align_bytes=64)
+        w_codes = const.tile([P, PASSES, GATE_COLS], U32, align_bytes=64)
+        w_scales = const.tile([P, PASSES, GATE_COLS], U8, align_bytes=64)
+        wh = const.tile([P, 2, GATE_COLS], BF16)
+        h0_rep = const.tile([P, SUBS, H], BF16)
+        h0_t = const.tile([P, SUBS, 2, P], BF16)
+        c0_rep = const.tile([P, SUBS, H], BF16)
+        c0 = const.tile([P, SUBS, H], F32)
+        state_term = const.tile([P, SUBS, GATE_COLS], F32)
+        zero_col = const.tile([P, 1], F32)
+        table_warm = const.tile([P, 1], F32)
+
+        x_tiles, xt_tiles, xg_tiles, code_tiles, scale_tiles = {}, {}, {}, {}, {}
+        acc_tiles, pre_tiles, act_tiles, fc_tiles, ig_tiles, hc_tiles, tanh_c_tiles = {}, {}, {}, {}, {}, {}, {}
+
+        def load_x(j):
+            x_sb = x_pool.tile([P, SUBS, D], BF16)
+            rows = x_rows[j * ROUND_ROWS : (j + 1) * ROUND_ROWS, :]
+            nc.sync.dma_start(out=x_sb[:], in_=rows.rearrange("(p r) k -> p r k", r=SUBS))
+            x_tiles[j] = x_sb
+
+        def load_w_piece(g, j):
+            rows = W[0, j, g * K_PASS : (g + 1) * K_PASS, :]
+            nc.sync.dma_start(
+                out=w_raw[:, g * GATES + j, :].rearrange("q (u e c) -> q u e c", u=2, e=2),
+                in_=rows.rearrange("(u q e) c -> q u e c", u=2, e=2),
+            )
+
+        def load_per_batch_row(dst, src):
+            span = P // SUBS
+            for a in range(SUBS):
+                nc.sync.dma_start(
+                    out=dst[a * span : (a + 1) * span, :, :],
+                    in_=src.rearrange("(p r) k -> p r k", r=SUBS),
+                )
+
+        def load_w_half(half):
+            for g in range(PASSES):
+                for j in range(half * GATES_PER_HALF, (half + 1) * GATES_PER_HALF):
+                    load_w_piece(g, j)
+
+        nc.vector.memset(b_row[:], 0.0)
+        nc.vector.memset(ones[:], 1.0)
+        nc.vector.memset(zero_col[:], 0.0)
+        make_identity(nc, ident[:])
+        nc.scalar.activation(out=table_warm[:], in_=zero_col[:], func=SIGMOID)
+
+        load_w_half(0)
+        load_x(0)
+        load_per_batch_row(h0_rep, h_0[0])
+        nc.sync.dma_start(out=b_row[0:1, :], in_=b.rearrange("l j c -> l (j c)"))
+        for e in range(2):
+            nc.sync.dma_start(
+                out=wh[:, e, :].rearrange("q (j c) -> q j c", j=GATES),
+                in_=W[0, :, D : D + H, :].rearrange("j (q e) c -> q e j c", e=2)[:, e],
+            )
+        load_w_half(1)
+        load_per_batch_row(c0_rep, c_0[0])
+        for j in range(1, X_BUFS):
+            load_x(j)
+
+        def regroup_views(g, j):
+            piece = g * GATES + j
+            src = w_raw[:, piece, :].rearrange("q (t c i) -> q c t i", t=PACK, i=4)
+            dst = w_grouped[:, piece, :].rearrange("q (c i t) -> q c t i", i=4, t=PACK)
+            return dst, src
+
+        def prepare_w_half(half):
+            first = half * GATES_PER_HALF
+            for g in range(PASSES):
+                dst, src = regroup_views(g, first)
+                nc.vector.tensor_copy(out=dst, in_=src)
+                dst, src = regroup_views(g, first + 1)
+                nc.scalar.copy(out=dst, in_=src)
+            for g in range(PASSES):
+                piece = g * GATES + first
+                cols = slice(half * BANK, (half + 1) * BANK)
+                nc.vector.quantize_mx(
+                    out=w_codes[:, g, cols].bitcast(FP8X4),
+                    scales=w_scales[:, g, cols],
+                    in_=w_grouped[:, piece : piece + GATES_PER_HALF, :].rearrange("q a n -> q (a n)"),
+                )
+
+        prepare_w_half(0)
+
+        h0_ps = psum_t.tile([P, WORDS // P, P], F32, name="xt")
+        for r in range(SUBS):
+            nc.tensor.transpose(out=h0_ps[:, r, :], in_=h0_rep[:, r, :].bitcast(F32), identity=ident[:])
+        for r in range(SUBS):
+            nc.vector.tensor_copy(
+                out=h0_t[:, r, :, :],
+                in_=h0_ps[:, r, :].bitcast(BF16).rearrange("q (m e) -> q e m", e=2),
+            )
+        for r in range(SUBS):
+            for half in range(HALVES):
+                cols = slice(half * BANK, (half + 1) * BANK)
+                acc = psum_g.tile([P, BANK], F32, name="acc")
+                nc.tensor.matmul(out=acc[:], lhsT=h0_t[:, r, 0, :], rhs=wh[:, 0, cols], start=True, stop=False)
+                nc.tensor.matmul(out=acc[:], lhsT=h0_t[:, r, 1, :], rhs=wh[:, 1, cols], start=False, stop=False)
+                nc.tensor.matmul(out=acc[:], lhsT=ones[:], rhs=b_row[:, cols], start=False, stop=True)
+                if half == 0:
+                    nc.vector.tensor_copy(out=state_term[:, r, cols], in_=acc[:])
+                else:
+                    nc.scalar.copy(out=state_term[:, r, cols], in_=acc[:])
+
+        prepare_w_half(1)
+        nc.vector.tensor_copy(out=c0[:], in_=c0_rep[:])
+
+        def transpose_x(j):
+            for r in range(SUBS):
+                xt = psum_t.tile([P, WORDS // P, P], F32, name="xt")
+                x_words = x_tiles[j][:, r, :].bitcast(F32)
+                for c in range(WORDS // P):
+                    nc.tensor.transpose(out=xt[:, c, :], in_=x_words[:, c * P : (c + 1) * P], identity=ident[:])
+                xt_tiles[j, r] = xt
+
+        def copy_x(j):
+            xg = work.tile([P, SUBS, D], BF16, align_bytes=64)
+            for r in range(SUBS):
+                nc.scalar.copy(
+                    out=xg[:, r, :].bitcast(F32).rearrange("q (g m u) -> q g m u", g=PASSES, u=2),
+                    in_=xt_tiles[j, r][:].rearrange("q (g u) m -> q g m u", u=2),
+                )
+            xg_tiles[j] = xg
+
+        def quantise_x(j):
+            x_codes = work.tile([P, SUBS * PASSES * P], U32, align_bytes=64)
+            x_scales = work.tile([P, SUBS * PASSES * P], U8, align_bytes=64)
+            nc.vector.quantize_mx(
+                out=x_codes[:].bitcast(FP8X4),
+                scales=x_scales[:],
+                in_=xg_tiles[j][:].rearrange("q r n -> q (r n)"),
+            )
+            code_tiles[j], scale_tiles[j] = x_codes, x_scales
+
+        def gate_matmuls(j):
+            for r in range(SUBS):
+                for half in range(HALVES):
+                    acc = psum_g.tile([P, BANK], F32, name="acc")
+                    for g in range(PASSES):
+                        m_cols = slice((r * PASSES + g) * P, (r * PASSES + g + 1) * P)
+                        n_cols = slice(half * BANK, (half + 1) * BANK)
+                        nc.tensor.matmul_mx(
+                            out=acc[:],
+                            lhsT=code_tiles[j][:, m_cols].bitcast(FP8X4),
+                            lhsT_scale=scale_tiles[j][:, m_cols],
+                            rhs=w_codes[:, g, n_cols].bitcast(FP8X4),
+                            rhs_scale=w_scales[:, g, n_cols],
+                            start=(g == 0),
+                            stop=(g == PASSES - 1),
+                        )
+                    acc_tiles[j, r, half] = acc
+
+        def add_state_term(j):
+            pre = work.tile([P, SUBS, GATE_COLS], F32)
+            for r in range(SUBS):
+                for half in range(HALVES):
+                    cols = slice(half * BANK, (half + 1) * BANK)
+                    nc.vector.tensor_tensor(
+                        out=pre[:, r, cols], in0=acc_tiles[j, r, half][:], in1=state_term[:, r, cols], op=ADD
+                    )
+            pre_tiles[j] = pre
+
+        def gate_functions(j):
+            pre = pre_tiles[j]
+            act = late.tile([P, SUBS, GATE_COLS], F32)
+            nc.scalar.activation(out=act[:, :, 0 : 2 * H], in_=pre[:, :, 0 : 2 * H], func=SIGMOID)
+            nc.scalar.activation(out=act[:, :, 2 * H : 3 * H], in_=pre[:, :, 2 * H : 3 * H], func=TANH)
+            nc.scalar.activation(out=act[:, :, 3 * H : 4 * H], in_=pre[:, :, 3 * H : 4 * H], func=SIGMOID)
+            act_tiles[j] = act
+
+        def gate_products(j):
+            act = act_tiles[j]
+            fc = work.tile([P, SUBS, H], F32)
+            ig = work.tile([P, SUBS, H], F32)
+            nc.gpsimd.tensor_tensor(out=fc[:], in0=act[:, :, 0:H], in1=c0[:], op=MULT)
+            nc.gpsimd.tensor_tensor(out=ig[:], in0=act[:, :, H : 2 * H], in1=act[:, :, 2 * H : 3 * H], op=MULT)
+            fc_tiles[j], ig_tiles[j] = fc, ig
+
+        def new_c(j):
+            hc = late.tile([P, 2, SUBS, H], F32)
+            nc.vector.tensor_tensor(out=hc[:, 1], in0=fc_tiles[j][:], in1=ig_tiles[j][:], op=ADD)
+            hc_tiles[j] = hc
+
+        def tanh_of_c(j):
+            tanh_c = work.tile([P, SUBS, H], F32)
+            nc.scalar.activation(out=tanh_c[:], in_=hc_tiles[j][:, 1], func=TANH)
+            tanh_c_tiles[j] = tanh_c
+
+        def new_h_and_store(j):
+            hc = hc_tiles[j]
+            o_gate = act_tiles[j][:, :, 3 * H : 4 * H]
+            nc.vector.tensor_tensor(out=hc[:, 0], in0=o_gate, in1=tanh_c_tiles[j][:], op=MULT)
+            rows = slice(j * ROUND_ROWS, (j + 1) * ROUND_ROWS)
+            nc.sync.dma_start(out=hc_rows[:, rows, :].rearrange("a (p r) h -> p a r h", r=SUBS), in_=hc[:])
+            nc.sync.dma_start(out=h_rows[rows, :].rearrange("(p r) h -> p r h", r=SUBS), in_=hc[:, 0])
+
+        def run(stage, j):
+            if 0 <= j < ROUNDS:
+                stage(j)
+
+        for i in range(-3, ROUNDS + 3):
+            run(tanh_of_c, i - 3)
+            run(quantise_x, i + 1)
+            run(gate_matmuls, i + 1)
+            run(add_state_term, i)
+            run(gate_functions, i - 1)
+            run(gate_products, i - 1)
+            run(new_c, i - 2)
+            run(new_h_and_store, i - 3)
+            run(transpose_x, i + 3)
+            run(load_x, i + 3 + X_BUFS)
+            run(copy_x, i + 2)

@@ -185,8 +185,8 @@ def tile_qlstm_t_kernel(tc, inputs, h_0, c_0, W, b, out_0, out_1):
             code_tiles[j], scale_tiles[j] = x_codes, x_scales
 
         def gate_matmuls(j):
-            for r in range(SUBS):
-                for half in range(HALVES):
+            for half in range(HALVES):
+                for r in range(SUBS):
                     acc = psum_g.tile([P, BANK], F32, name="acc")
                     for g in range(PASSES):
                         m_cols = slice((r * PASSES + g) * P, (r * PASSES + g + 1) * P)
@@ -204,8 +204,8 @@ def tile_qlstm_t_kernel(tc, inputs, h_0, c_0, W, b, out_0, out_1):
 
         def add_state_term(j):
             pre = work.tile([P, SUBS, GATE_COLS], F32)
-            for r in range(SUBS):
-                for half in range(HALVES):
+            for half in range(HALVES):
+                for r in range(SUBS):
                     cols = slice(half * BANK, (half + 1) * BANK)
                     nc.vector.tensor_tensor(
                         out=pre[:, r, cols], in0=acc_tiles[j, r, half][:], in1=state_term[:, r, cols], op=ADD
@@ -216,16 +216,16 @@ def tile_qlstm_t_kernel(tc, inputs, h_0, c_0, W, b, out_0, out_1):
             pre = pre_tiles[j]
             act = late.tile([P, SUBS, GATE_COLS], F32)
             nc.scalar.activation(out=act[:, :, 0 : 2 * H], in_=pre[:, :, 0 : 2 * H], func=SIGMOID)
-            nc.scalar.activation(out=act[:, :, 2 * H : 3 * H], in_=pre[:, :, 2 * H : 3 * H], func=TANH)
             nc.scalar.activation(out=act[:, :, 3 * H : 4 * H], in_=pre[:, :, 3 * H : 4 * H], func=SIGMOID)
+            nc.scalar.activation(out=act[:, :, 2 * H : 3 * H], in_=pre[:, :, 2 * H : 3 * H], func=TANH)
             act_tiles[j] = act
 
         def gate_products(j):
             act = act_tiles[j]
             fc = work.tile([P, SUBS, H], F32)
             ig = work.tile([P, SUBS, H], F32)
-            nc.gpsimd.tensor_tensor(out=fc[:], in0=act[:, :, 0:H], in1=c0[:], op=MULT)
             nc.gpsimd.tensor_tensor(out=ig[:], in0=act[:, :, H : 2 * H], in1=act[:, :, 2 * H : 3 * H], op=MULT)
+            nc.gpsimd.tensor_tensor(out=fc[:], in0=act[:, :, 0:H], in1=c0[:], op=MULT)
             fc_tiles[j], ig_tiles[j] = fc, ig
 
         def new_c(j):
@@ -250,15 +250,16 @@ def tile_qlstm_t_kernel(tc, inputs, h_0, c_0, W, b, out_0, out_1):
             if 0 <= j < ROUNDS:
                 stage(j)
 
-        for i in range(-3, ROUNDS + 3):
-            run(tanh_of_c, i - 3)
-            run(quantise_x, i + 1)
-            run(gate_matmuls, i + 1)
-            run(add_state_term, i)
-            run(gate_functions, i - 1)
-            run(gate_products, i - 1)
-            run(new_c, i - 2)
-            run(new_h_and_store, i - 3)
-            run(transpose_x, i + 3)
-            run(load_x, i + 3 + X_BUFS)
-            run(copy_x, i + 2)
+        with tc.manual_schedule():
+            for i in range(-3, ROUNDS + 2):
+                run(tanh_of_c, i - 2)
+                run(copy_x, i + 2)
+                run(gate_matmuls, i + 1)
+                run(add_state_term, i)
+                run(gate_functions, i)
+                run(gate_products, i - 1)
+                run(quantise_x, i + 2)
+                run(new_c, i - 1)
+                run(new_h_and_store, i - 2)
+                run(transpose_x, i + 3)
+                run(load_x, i + 3 + X_BUFS)

@@ -23,19 +23,18 @@ BANK = 512
 HALVES = GATE_COLS // BANK
 GATES_PER_HALF = GATES // HALVES
 SUBS = 2
-ROUND_ROWS = SUBS * P
-ROUNDS = T * B // ROUND_ROWS
+ROUNDS = T // SUBS
 WORDS = D // 2
 X_BUFS = 6
+CG_BUFS = 2
+PINNED_FROM = 2
 
 FLOPS = 2 * T * B * D * GATE_COLS + 2 * B * H * GATE_COLS
 
 
 def tile_qlstm_t_kernel(tc, inputs, h_0, c_0, W, b, out_0, out_1):
     nc = tc.nc
-    x_rows = inputs.flatten_outer_dims()
-    h_rows = out_0.flatten_outer_dims()
-    hc_rows = out_1.rearrange("a t l n h -> a (t l n) h")
+    hc_steps = out_1.rearrange("a t l n h -> a (t l) n h")
 
     with ExitStack() as stack:
         const = stack.enter_context(tc.tile_pool(name="const", bufs=1))
@@ -53,21 +52,20 @@ def tile_qlstm_t_kernel(tc, inputs, h_0, c_0, W, b, out_0, out_1):
         w_codes = const.tile([P, PASSES, GATE_COLS], U32, align_bytes=64)
         w_scales = const.tile([P, PASSES, GATE_COLS], U8, align_bytes=64)
         wh = const.tile([P, 2, GATE_COLS], BF16)
-        h0_rep = const.tile([P, SUBS, H], BF16)
-        h0_t = const.tile([P, SUBS, 2, P], BF16)
-        c0_rep = const.tile([P, SUBS, H], BF16)
-        c0 = const.tile([P, SUBS, H], F32)
-        state_term = const.tile([P, SUBS, GATE_COLS], F32)
+        h0_sb = const.tile([P, H], BF16)
+        h0_t = const.tile([P, 2, P], BF16)
+        c0_sb = const.tile([P, H], BF16)
+        cg_bufs = [const.tile([P, SUBS, 2 * H], F32, name="cg%d" % n) for n in range(CG_BUFS)]
+        state_term = const.tile([P, GATE_COLS], F32)
         zero_col = const.tile([P, 1], F32)
         table_warm = const.tile([P, 1], F32)
 
         x_tiles, xt_tiles, xg_tiles, code_tiles, scale_tiles = {}, {}, {}, {}, {}
-        acc_tiles, pre_tiles, act_tiles, fc_tiles, ig_tiles, hc_tiles, tanh_c_tiles = {}, {}, {}, {}, {}, {}, {}
+        acc_tiles, pre_tiles, act_tiles, fc_ig_tiles, hc_tiles, tanh_c_tiles = {}, {}, {}, {}, {}, {}
 
         def load_x(j):
             x_sb = x_pool.tile([P, SUBS, D], BF16)
-            rows = x_rows[j * ROUND_ROWS : (j + 1) * ROUND_ROWS, :]
-            nc.sync.dma_start(out=x_sb[:], in_=rows.rearrange("(p r) k -> p r k", r=SUBS))
+            nc.sync.dma_start(out=x_sb[:], in_=inputs[j * SUBS : (j + 1) * SUBS].rearrange("r p k -> p r k"))
             x_tiles[j] = x_sb
 
         def load_w_piece(g, j):
@@ -76,14 +74,6 @@ def tile_qlstm_t_kernel(tc, inputs, h_0, c_0, W, b, out_0, out_1):
                 out=w_raw[:, g * GATES + j, :].rearrange("q (u e c) -> q u e c", u=2, e=2),
                 in_=rows.rearrange("(u q e) c -> q u e c", u=2, e=2),
             )
-
-        def load_per_batch_row(dst, src):
-            span = P // SUBS
-            for a in range(SUBS):
-                nc.sync.dma_start(
-                    out=dst[a * span : (a + 1) * span, :, :],
-                    in_=src.rearrange("(p r) k -> p r k", r=SUBS),
-                )
 
         def load_w_half(half):
             for g in range(PASSES):
@@ -98,16 +88,17 @@ def tile_qlstm_t_kernel(tc, inputs, h_0, c_0, W, b, out_0, out_1):
 
         load_w_half(0)
         load_x(0)
-        load_per_batch_row(h0_rep, h_0[0])
+        nc.sync.dma_start(out=h0_sb[:], in_=h_0[0])
         nc.sync.dma_start(out=b_row[0:1, :], in_=b.rearrange("l j c -> l (j c)"))
         for e in range(2):
             nc.sync.dma_start(
                 out=wh[:, e, :].rearrange("q (j c) -> q j c", j=GATES),
                 in_=W[0, :, D : D + H, :].rearrange("j (q e) c -> q e j c", e=2)[:, e],
             )
+        load_x(1)
         load_w_half(1)
-        load_per_batch_row(c0_rep, c_0[0])
-        for j in range(1, X_BUFS):
+        nc.sync.dma_start(out=c0_sb[:], in_=c_0[0])
+        for j in range(2, X_BUFS):
             load_x(j)
 
         def regroup_views(g, j):
@@ -118,14 +109,13 @@ def tile_qlstm_t_kernel(tc, inputs, h_0, c_0, W, b, out_0, out_1):
 
         def prepare_w_half(half):
             first = half * GATES_PER_HALF
+            cols = slice(half * BANK, (half + 1) * BANK)
             for g in range(PASSES):
                 dst, src = regroup_views(g, first)
-                nc.vector.tensor_copy(out=dst, in_=src)
-                dst, src = regroup_views(g, first + 1)
                 nc.scalar.copy(out=dst, in_=src)
-            for g in range(PASSES):
+                dst, src = regroup_views(g, first + 1)
+                nc.vector.tensor_copy(out=dst, in_=src)
                 piece = g * GATES + first
-                cols = slice(half * BANK, (half + 1) * BANK)
                 nc.vector.quantize_mx(
                     out=w_codes[:, g, cols].bitcast(FP8X4),
                     scales=w_scales[:, g, cols],
@@ -135,27 +125,22 @@ def tile_qlstm_t_kernel(tc, inputs, h_0, c_0, W, b, out_0, out_1):
         prepare_w_half(0)
 
         h0_ps = psum_t.tile([P, WORDS // P, P], F32, name="xt")
-        for r in range(SUBS):
-            nc.tensor.transpose(out=h0_ps[:, r, :], in_=h0_rep[:, r, :].bitcast(F32), identity=ident[:])
-        for r in range(SUBS):
-            nc.vector.tensor_copy(
-                out=h0_t[:, r, :, :],
-                in_=h0_ps[:, r, :].bitcast(BF16).rearrange("q (m e) -> q e m", e=2),
-            )
-        for r in range(SUBS):
-            for half in range(HALVES):
-                cols = slice(half * BANK, (half + 1) * BANK)
-                acc = psum_g.tile([P, BANK], F32, name="acc")
-                nc.tensor.matmul(out=acc[:], lhsT=h0_t[:, r, 0, :], rhs=wh[:, 0, cols], start=True, stop=False)
-                nc.tensor.matmul(out=acc[:], lhsT=h0_t[:, r, 1, :], rhs=wh[:, 1, cols], start=False, stop=False)
-                nc.tensor.matmul(out=acc[:], lhsT=ones[:], rhs=b_row[:, cols], start=False, stop=True)
-                if half == 0:
-                    nc.vector.tensor_copy(out=state_term[:, r, cols], in_=acc[:])
-                else:
-                    nc.scalar.copy(out=state_term[:, r, cols], in_=acc[:])
+        nc.tensor.transpose(out=h0_ps[:, 0, :], in_=h0_sb[:].bitcast(F32), identity=ident[:])
+        nc.vector.tensor_copy(out=h0_t[:], in_=h0_ps[:, 0, :].bitcast(BF16).rearrange("q (m e) -> q e m", e=2))
+        for half in range(HALVES):
+            cols = slice(half * BANK, (half + 1) * BANK)
+            acc = psum_g.tile([P, BANK], F32, name="acc")
+            nc.tensor.matmul(out=acc[:], lhsT=h0_t[:, 0, :], rhs=wh[:, 0, cols], start=True, stop=False)
+            nc.tensor.matmul(out=acc[:], lhsT=h0_t[:, 1, :], rhs=wh[:, 1, cols], start=False, stop=False)
+            nc.tensor.matmul(out=acc[:], lhsT=ones[:], rhs=b_row[:, cols], start=False, stop=True)
+            if half == 0:
+                nc.vector.tensor_copy(out=state_term[:, cols], in_=acc[:])
+            else:
+                nc.scalar.copy(out=state_term[:, cols], in_=acc[:])
 
         prepare_w_half(1)
-        nc.vector.tensor_copy(out=c0[:], in_=c0_rep[:])
+        for cg in cg_bufs:
+            nc.vector.tensor_copy(out=cg[:, :, 0:H], in_=c0_sb[:].unsqueeze(1).to_broadcast([P, SUBS, H]))
 
         def transpose_x(j):
             for r in range(SUBS):
@@ -208,29 +193,34 @@ def tile_qlstm_t_kernel(tc, inputs, h_0, c_0, W, b, out_0, out_1):
                 for r in range(SUBS):
                     cols = slice(half * BANK, (half + 1) * BANK)
                     nc.vector.tensor_tensor(
-                        out=pre[:, r, cols], in0=acc_tiles[j, r, half][:], in1=state_term[:, r, cols], op=ADD
+                        out=pre[:, r, cols], in0=acc_tiles[j, r, half][:], in1=state_term[:, cols], op=ADD
                     )
             pre_tiles[j] = pre
 
         def gate_functions(j):
             pre = pre_tiles[j]
-            act = late.tile([P, SUBS, GATE_COLS], F32)
+            act = late.tile([P, SUBS, 3 * H], F32)
             nc.scalar.activation(out=act[:, :, 0 : 2 * H], in_=pre[:, :, 0 : 2 * H], func=SIGMOID)
-            nc.scalar.activation(out=act[:, :, 3 * H : 4 * H], in_=pre[:, :, 3 * H : 4 * H], func=SIGMOID)
-            nc.scalar.activation(out=act[:, :, 2 * H : 3 * H], in_=pre[:, :, 2 * H : 3 * H], func=TANH)
+            g_gate = (cg_bufs[j % CG_BUFS][:, :, H : 2 * H], pre[:, :, 2 * H : 3 * H], TANH)
+            o_gate = (act[:, :, 2 * H : 3 * H], pre[:, :, 3 * H : 4 * H], SIGMOID)
+            for dst, src, func in (g_gate, o_gate) if j == ROUNDS - 1 else (o_gate, g_gate):
+                nc.scalar.activation(out=dst, in_=src, func=func)
             act_tiles[j] = act
 
         def gate_products(j):
-            act = act_tiles[j]
-            fc = work.tile([P, SUBS, H], F32)
-            ig = work.tile([P, SUBS, H], F32)
-            nc.gpsimd.tensor_tensor(out=ig[:], in0=act[:, :, H : 2 * H], in1=act[:, :, 2 * H : 3 * H], op=MULT)
-            nc.gpsimd.tensor_tensor(out=fc[:], in0=act[:, :, 0:H], in1=c0[:], op=MULT)
-            fc_tiles[j], ig_tiles[j] = fc, ig
+            engine = nc.vector if j == ROUNDS - 1 else nc.gpsimd
+            fc_ig = work.tile([P, SUBS, 2 * H], F32)
+            engine.tensor_tensor(out=fc_ig[:], in0=act_tiles[j][:, :, 0 : 2 * H], in1=cg_bufs[j % CG_BUFS][:], op=MULT)
+            fc_ig_tiles[j] = fc_ig
+
+        def store(dram_steps, j, tile_rows):
+            nc.sync.dma_start(out=dram_steps[j * SUBS : (j + 1) * SUBS].rearrange("r p h -> p r h"), in_=tile_rows)
 
         def new_c(j):
             hc = late.tile([P, 2, SUBS, H], F32)
-            nc.vector.tensor_tensor(out=hc[:, 1], in0=fc_tiles[j][:], in1=ig_tiles[j][:], op=ADD)
+            fc_ig = fc_ig_tiles[j]
+            nc.vector.tensor_tensor(out=hc[:, 1], in0=fc_ig[:, :, 0:H], in1=fc_ig[:, :, H : 2 * H], op=ADD)
+            store(hc_steps[1], j, hc[:, 1])
             hc_tiles[j] = hc
 
         def tanh_of_c(j):
@@ -240,26 +230,30 @@ def tile_qlstm_t_kernel(tc, inputs, h_0, c_0, W, b, out_0, out_1):
 
         def new_h_and_store(j):
             hc = hc_tiles[j]
-            o_gate = act_tiles[j][:, :, 3 * H : 4 * H]
+            o_gate = act_tiles[j][:, :, 2 * H : 3 * H]
             nc.vector.tensor_tensor(out=hc[:, 0], in0=o_gate, in1=tanh_c_tiles[j][:], op=MULT)
-            rows = slice(j * ROUND_ROWS, (j + 1) * ROUND_ROWS)
-            nc.sync.dma_start(out=hc_rows[:, rows, :].rearrange("a (p r) h -> p a r h", r=SUBS), in_=hc[:])
-            nc.sync.dma_start(out=h_rows[rows, :].rearrange("(p r) h -> p r h", r=SUBS), in_=hc[:, 0])
+            store(hc_steps[0], j, hc[:, 0])
+            store(out_0, j, hc[:, 0])
 
         def run(stage, j):
             if 0 <= j < ROUNDS:
                 stage(j)
 
+        def step(i):
+            run(tanh_of_c, i - 2)
+            run(copy_x, i + 2)
+            run(gate_matmuls, i + 1)
+            run(add_state_term, i)
+            run(gate_functions, i)
+            run(gate_products, i - 1)
+            run(quantise_x, i + 2)
+            run(new_c, i - 1)
+            run(new_h_and_store, i - 2)
+            run(transpose_x, i + 3)
+            run(load_x, i + 3 + X_BUFS)
+
+        for i in range(-3, PINNED_FROM):
+            step(i)
         with tc.manual_schedule():
-            for i in range(-3, ROUNDS + 2):
-                run(tanh_of_c, i - 2)
-                run(copy_x, i + 2)
-                run(gate_matmuls, i + 1)
-                run(add_state_term, i)
-                run(gate_functions, i)
-                run(gate_products, i - 1)
-                run(quantise_x, i + 2)
-                run(new_c, i - 1)
-                run(new_h_and_store, i - 2)
-                run(transpose_x, i + 3)
-                run(load_x, i + 3 + X_BUFS)
+            for i in range(PINNED_FROM, ROUNDS + 2):
+                step(i)

@@ -56,12 +56,13 @@ def tile_qlstm_t_kernel(tc, inputs, h_0, c_0, W, b, out_0, out_1):
         h0_t = const.tile([P, 2, P], BF16)
         c0_sb = const.tile([P, H], BF16)
         cg_bufs = [const.tile([P, SUBS, 2 * H], F32, name="cg%d" % n) for n in range(CG_BUFS)]
+        fc_ig = const.tile([P, SUBS, 2 * H], F32)
         state_term = const.tile([P, GATE_COLS], F32)
         zero_col = const.tile([P, 1], F32)
         table_warm = const.tile([P, 1], F32)
 
         x_tiles, xt_tiles, xg_tiles, code_tiles, scale_tiles = {}, {}, {}, {}, {}
-        acc_tiles, pre_tiles, act_tiles, fc_ig_tiles, hc_tiles, tanh_c_tiles = {}, {}, {}, {}, {}, {}
+        acc_tiles, pre_tiles, act_tiles, hc_tiles, tanh_c_tiles = {}, {}, {}, {}, {}
 
         def load_x(j):
             x_sb = x_pool.tile([P, SUBS, D], BF16)
@@ -209,16 +210,13 @@ def tile_qlstm_t_kernel(tc, inputs, h_0, c_0, W, b, out_0, out_1):
 
         def gate_products(j):
             engine = nc.vector if j == ROUNDS - 1 else nc.gpsimd
-            fc_ig = work.tile([P, SUBS, 2 * H], F32)
             engine.tensor_tensor(out=fc_ig[:], in0=act_tiles[j][:, :, 0 : 2 * H], in1=cg_bufs[j % CG_BUFS][:], op=MULT)
-            fc_ig_tiles[j] = fc_ig
 
         def store(dram_steps, j, tile_rows):
             nc.sync.dma_start(out=dram_steps[j * SUBS : (j + 1) * SUBS].rearrange("r p h -> p r h"), in_=tile_rows)
 
         def new_c(j):
             hc = late.tile([P, 2, SUBS, H], F32)
-            fc_ig = fc_ig_tiles[j]
             nc.vector.tensor_tensor(out=hc[:, 1], in0=fc_ig[:, :, 0:H], in1=fc_ig[:, :, H : 2 * H], op=ADD)
             store(hc_steps[1], j, hc[:, 1])
             hc_tiles[j] = hc
@@ -240,15 +238,15 @@ def tile_qlstm_t_kernel(tc, inputs, h_0, c_0, W, b, out_0, out_1):
                 stage(j)
 
         def step(i):
-            run(tanh_of_c, i - 2)
             run(copy_x, i + 2)
+            run(tanh_of_c, i - 2)
             run(gate_matmuls, i + 1)
             run(add_state_term, i)
             run(gate_functions, i)
             run(gate_products, i - 1)
             run(quantise_x, i + 2)
-            run(new_c, i - 1)
             run(new_h_and_store, i - 2)
+            run(new_c, i - 1)
             run(transpose_x, i + 3)
             run(load_x, i + 3 + X_BUFS)
 

@@ -56,13 +56,12 @@ def tile_qlstm_t_kernel(tc, inputs, h_0, c_0, W, b, out_0, out_1):
         h0_t = const.tile([P, 2, P], BF16)
         c0_sb = const.tile([P, H], BF16)
         cg_bufs = [const.tile([P, SUBS, 2 * H], F32, name="cg%d" % n) for n in range(CG_BUFS)]
-        fc_ig = const.tile([P, SUBS, 2 * H], F32)
         state_term = const.tile([P, GATE_COLS], F32)
         zero_col = const.tile([P, 1], F32)
         table_warm = const.tile([P, 1], F32)
 
         x_tiles, xt_tiles, xg_tiles, code_tiles, scale_tiles = {}, {}, {}, {}, {}
-        acc_tiles, pre_tiles, act_tiles, hc_tiles, tanh_c_tiles = {}, {}, {}, {}, {}
+        acc_tiles, pre_tiles, act_tiles, fc_ig_tiles, hc_tiles, tanh_c_tiles = {}, {}, {}, {}, {}, {}
 
         def load_x(j):
             x_sb = x_pool.tile([P, SUBS, D], BF16)
@@ -91,6 +90,7 @@ def tile_qlstm_t_kernel(tc, inputs, h_0, c_0, W, b, out_0, out_1):
         load_x(0)
         nc.sync.dma_start(out=h0_sb[:], in_=h_0[0])
         nc.sync.dma_start(out=b_row[0:1, :], in_=b.rearrange("l j c -> l (j c)"))
+        nc.sync.dma_start(out=c0_sb[:], in_=c_0[0])
         for e in range(2):
             nc.sync.dma_start(
                 out=wh[:, e, :].rearrange("q (j c) -> q j c", j=GATES),
@@ -98,7 +98,6 @@ def tile_qlstm_t_kernel(tc, inputs, h_0, c_0, W, b, out_0, out_1):
             )
         load_x(1)
         load_w_half(1)
-        nc.sync.dma_start(out=c0_sb[:], in_=c_0[0])
         for j in range(2, X_BUFS):
             load_x(j)
 
@@ -202,21 +201,22 @@ def tile_qlstm_t_kernel(tc, inputs, h_0, c_0, W, b, out_0, out_1):
             pre = pre_tiles[j]
             act = late.tile([P, SUBS, 3 * H], F32)
             nc.scalar.activation(out=act[:, :, 0 : 2 * H], in_=pre[:, :, 0 : 2 * H], func=SIGMOID)
-            g_gate = (cg_bufs[j % CG_BUFS][:, :, H : 2 * H], pre[:, :, 2 * H : 3 * H], TANH)
-            o_gate = (act[:, :, 2 * H : 3 * H], pre[:, :, 3 * H : 4 * H], SIGMOID)
-            for dst, src, func in (g_gate, o_gate) if j == ROUNDS - 1 else (o_gate, g_gate):
-                nc.scalar.activation(out=dst, in_=src, func=func)
+            nc.scalar.activation(out=cg_bufs[j % CG_BUFS][:, :, H : 2 * H], in_=pre[:, :, 2 * H : 3 * H], func=TANH)
+            nc.scalar.activation(out=act[:, :, 2 * H : 3 * H], in_=pre[:, :, 3 * H : 4 * H], func=SIGMOID)
             act_tiles[j] = act
 
         def gate_products(j):
             engine = nc.vector if j == ROUNDS - 1 else nc.gpsimd
+            fc_ig = work.tile([P, SUBS, 2 * H], F32)
             engine.tensor_tensor(out=fc_ig[:], in0=act_tiles[j][:, :, 0 : 2 * H], in1=cg_bufs[j % CG_BUFS][:], op=MULT)
+            fc_ig_tiles[j] = fc_ig
 
         def store(dram_steps, j, tile_rows):
             nc.sync.dma_start(out=dram_steps[j * SUBS : (j + 1) * SUBS].rearrange("r p h -> p r h"), in_=tile_rows)
 
         def new_c(j):
             hc = late.tile([P, 2, SUBS, H], F32)
+            fc_ig = fc_ig_tiles[j]
             nc.vector.tensor_tensor(out=hc[:, 1], in0=fc_ig[:, :, 0:H], in1=fc_ig[:, :, H : 2 * H], op=ADD)
             store(hc_steps[1], j, hc[:, 1])
             hc_tiles[j] = hc
@@ -238,15 +238,15 @@ def tile_qlstm_t_kernel(tc, inputs, h_0, c_0, W, b, out_0, out_1):
                 stage(j)
 
         def step(i):
-            run(copy_x, i + 2)
             run(tanh_of_c, i - 2)
+            run(copy_x, i + 2)
             run(gate_matmuls, i + 1)
             run(add_state_term, i)
             run(gate_functions, i)
             run(gate_products, i - 1)
             run(quantise_x, i + 2)
-            run(new_h_and_store, i - 2)
             run(new_c, i - 1)
+            run(new_h_and_store, i - 2)
             run(transpose_x, i + 3)
             run(load_x, i + 3 + X_BUFS)
 

from contextlib import ExitStack

import concourse.mybir as mybir
from concourse.masks import make_identity

F32 = mybir.dt.float32
BF16 = mybir.dt.bfloat16
U32 = mybir.dt.uint32
U8 = mybir.dt.uint8
FP8X4 = mybir.dt.float8_e4m3fn_x4
SIGMOID = mybir.ActivationFunctionType.Sigmoid
TANH = mybir.ActivationFunctionType.Tanh
ADD = mybir.AluOpType.add
MULT = mybir.AluOpType.mult

T, B, D, H, GATES = 32, 128, 1024, 256, 4
P = 128
PACK = 4
K_PASS = P * PACK
PASSES = D // K_PASS
GATE_COLS = GATES * H
BANK = 512
HALVES = GATE_COLS // BANK
GATES_PER_HALF = GATES // HALVES
SUBS = 2
ROUNDS = T // SUBS
WORDS = D // 2
X_BUFS = 6
CG_BUFS = 2
PINNED_FROM = 2

FLOPS = 2 * T * B * D * GATE_COLS + 2 * B * H * GATE_COLS


def tile_qlstm_t_kernel(tc, inputs, h_0, c_0, W, b, out_0, out_1):
    nc = tc.nc
    hc_steps = out_1.rearrange("a t l n h -> a (t l) n h")

    with ExitStack() as stack:
        const = stack.enter_context(tc.tile_pool(name="const", bufs=1))
        x_pool = stack.enter_context(tc.tile_pool(name="x_pool", bufs=X_BUFS))
        work = stack.enter_context(tc.tile_pool(name="work", bufs=3))
        late = stack.enter_context(tc.tile_pool(name="late", bufs=4))
        psum_t = stack.enter_context(tc.psum_pool(name="psum_t", bufs=2))
        psum_g = stack.enter_context(tc.psum_pool(name="psum_g", bufs=6))

        ident = const.tile([P, P], F32)
        ones = const.tile([P, P], BF16)
        b_row = const.tile([P, GATE_COLS], BF16)
        w_raw = const.tile([P, PASSES * GATES, PACK * H], BF16)
        w_grouped = const.tile([P, PASSES * GATES, H * PACK], BF16, align_bytes=64)
        w_codes = const.tile([P, PASSES, GATE_COLS], U32, align_bytes=64)
        w_scales = const.tile([P, PASSES, GATE_COLS], U8, align_bytes=64)
        wh = const.tile([P, 2, GATE_COLS], BF16)
        h0_sb = const.tile([P, H], BF16)
        h0_t = const.tile([P, 2, P], BF16)
        c0_sb = const.tile([P, H], BF16)
        cg_bufs = [const.tile([P, SUBS, 2 * H], F32, name="cg%d" % n) for n in range(CG_BUFS)]
        state_term = const.tile([P, GATE_COLS], F32)
        zero_col = const.tile([P, 1], F32)
        table_warm = const.tile([P, 1], F32)

        x_tiles, xt_tiles, xg_tiles, code_tiles, scale_tiles = {}, {}, {}, {}, {}
        acc_tiles, pre_tiles, act_tiles, fc_ig_tiles, hc_tiles, tanh_c_tiles = {}, {}, {}, {}, {}, {}

        def load_x(j):
            x_sb = x_pool.tile([P, SUBS, D], BF16)
            nc.sync.dma_start(out=x_sb[:], in_=inputs[j * SUBS : (j + 1) * SUBS].rearrange("r p k -> p r k"))
            x_tiles[j] = x_sb

        def load_w_piece(g, j):
            rows = W[0, j, g * K_PASS : (g + 1) * K_PASS, :]
            nc.sync.dma_start(
                out=w_raw[:, g * GATES + j, :].rearrange("q (u e c) -> q u e c", u=2, e=2),
                in_=rows.rearrange("(u q e) c -> q u e c", u=2, e=2),
            )

        def load_w_half(half):
            for g in range(PASSES):
                for j in range(half * GATES_PER_HALF, (half + 1) * GATES_PER_HALF):
                    load_w_piece(g, j)

        nc.vector.memset(b_row[:], 0.0)
        nc.vector.memset(ones[:], 1.0)
        nc.vector.memset(zero_col[:], 0.0)
        make_identity(nc, ident[:])
        nc.scalar.activation(out=table_warm[:], in_=zero_col[:], func=SIGMOID)

        load_w_half(0)
        load_x(0)
        nc.sync.dma_start(out=h0_sb[:], in_=h_0[0])
        nc.sync.dma_start(out=b_row[0:1, :], in_=b.rearrange("l j c -> l (j c)"))
        nc.sync.dma_start(out=c0_sb[:], in_=c_0[0])
        for e in range(2):
            nc.sync.dma_start(
                out=wh[:, e, :].rearrange("q (j c) -> q j c", j=GATES),
                in_=W[0, :, D : D + H, :].rearrange("j (q e) c -> q e j c", e=2)[:, e],
            )
        load_x(1)
        load_w_half(1)
        for j in range(2, X_BUFS):
            load_x(j)

        def regroup_views(g, j):
            piece = g * GATES + j
            src = w_raw[:, piece, :].rearrange("q (t c i) -> q c t i", t=PACK, i=4)
            dst = w_grouped[:, piece, :].rearrange("q (c i t) -> q c t i", i=4, t=PACK)
            return dst, src

        def prepare_w_half(half):
            first = half * GATES_PER_HALF
            cols = slice(half * BANK, (half + 1) * BANK)
            for g in range(PASSES):
                dst, src = regroup_views(g, first)
                nc.scalar.copy(out=dst, in_=src)
                dst, src = regroup_views(g, first + 1)
                nc.vector.tensor_copy(out=dst, in_=src)
                piece = g * GATES + first
                nc.vector.quantize_mx(
                    out=w_codes[:, g, cols].bitcast(FP8X4),
                    scales=w_scales[:, g, cols],
                    in_=w_grouped[:, piece : piece + GATES_PER_HALF, :].rearrange("q a n -> q (a n)"),
                )

        prepare_w_half(0)

        h0_ps = psum_t.tile([P, WORDS // P, P], F32, name="xt")
        nc.tensor.transpose(out=h0_ps[:, 0, :], in_=h0_sb[:].bitcast(F32), identity=ident[:])
        nc.vector.tensor_copy(out=h0_t[:], in_=h0_ps[:, 0, :].bitcast(BF16).rearrange("q (m e) -> q e m", e=2))
        for half in range(HALVES):
            cols = slice(half * BANK, (half + 1) * BANK)
            acc = psum_g.tile([P, BANK], F32, name="acc")
            nc.tensor.matmul(out=acc[:], lhsT=h0_t[:, 0, :], rhs=wh[:, 0, cols], start=True, stop=False)
            nc.tensor.matmul(out=acc[:], lhsT=h0_t[:, 1, :], rhs=wh[:, 1, cols], start=False, stop=False)
            nc.tensor.matmul(out=acc[:], lhsT=ones[:], rhs=b_row[:, cols], start=False, stop=True)
            if half == 0:
                nc.vector.tensor_copy(out=state_term[:, cols], in_=acc[:])
            else:
                nc.scalar.copy(out=state_term[:, cols], in_=acc[:])

        prepare_w_half(1)
        for cg in cg_bufs:
            nc.vector.tensor_copy(out=cg[:, :, 0:H], in_=c0_sb[:].unsqueeze(1).to_broadcast([P, SUBS, H]))

        def transpose_x(j):
            for r in range(SUBS):
                xt = psum_t.tile([P, WORDS // P, P], F32, name="xt")
                x_words = x_tiles[j][:, r, :].bitcast(F32)
                for c in range(WORDS // P):
                    nc.tensor.transpose(out=xt[:, c, :], in_=x_words[:, c * P : (c + 1) * P], identity=ident[:])
                xt_tiles[j, r] = xt

        def copy_x(j):
            xg = work.tile([P, SUBS, D], BF16, align_bytes=64)
            for r in range(SUBS):
                nc.scalar.copy(
                    out=xg[:, r, :].bitcast(F32).rearrange("q (g m u) -> q g m u", g=PASSES, u=2),
                    in_=xt_tiles[j, r][:].rearrange("q (g u) m -> q g m u", u=2),
                )
            xg_tiles[j] = xg

        def quantise_x(j):
            x_codes = work.tile([P, SUBS * PASSES * P], U32, align_bytes=64)
            x_scales = work.tile([P, SUBS * PASSES * P], U8, align_bytes=64)
            nc.vector.quantize_mx(
                out=x_codes[:].bitcast(FP8X4),
                scales=x_scales[:],
                in_=xg_tiles[j][:].rearrange("q r n -> q (r n)"),
            )
            code_tiles[j], scale_tiles[j] = x_codes, x_scales

        def gate_matmuls(j):
            for half in range(HALVES):
                for r in range(SUBS):
                    acc = psum_g.tile([P, BANK], F32, name="acc")
                    for g in range(PASSES):
                        m_cols = slice((r * PASSES + g) * P, (r * PASSES + g + 1) * P)
                        n_cols = slice(half * BANK, (half + 1) * BANK)
                        nc.tensor.matmul_mx(
                            out=acc[:],
                            lhsT=code_tiles[j][:, m_cols].bitcast(FP8X4),
                            lhsT_scale=scale_tiles[j][:, m_cols],
                            rhs=w_codes[:, g, n_cols].bitcast(FP8X4),
                            rhs_scale=w_scales[:, g, n_cols],
                            start=(g == 0),
                            stop=(g == PASSES - 1),
                        )
                    acc_tiles[j, r, half] = acc

        def add_state_term(j):
            pre = work.tile([P, SUBS, GATE_COLS], F32)
            for half in range(HALVES):
                for r in range(SUBS):
                    cols = slice(half * BANK, (half + 1) * BANK)
                    nc.vector.tensor_tensor(
                        out=pre[:, r, cols], in0=acc_tiles[j, r, half][:], in1=state_term[:, cols], op=ADD
                    )
            pre_tiles[j] = pre

        def gate_functions(j):
            pre = pre_tiles[j]
            act = late.tile([P, SUBS, 3 * H], F32)
            nc.scalar.activation(out=act[:, :, 0 : 2 * H], in_=pre[:, :, 0 : 2 * H], func=SIGMOID)
            nc.scalar.activation(out=cg_bufs[j % CG_BUFS][:, :, H : 2 * H], in_=pre[:, :, 2 * H : 3 * H], func=TANH)
            nc.scalar.activation(out=act[:, :, 2 * H : 3 * H], in_=pre[:, :, 3 * H : 4 * H], func=SIGMOID)
            act_tiles[j] = act

        def gate_products(j):
            engine = nc.vector if j == ROUNDS - 1 else nc.gpsimd
            fc_ig = work.tile([P, SUBS, 2 * H], F32)
            engine.tensor_tensor(out=fc_ig[:], in0=act_tiles[j][:, :, 0 : 2 * H], in1=cg_bufs[j % CG_BUFS][:], op=MULT)
            fc_ig_tiles[j] = fc_ig

        def store(dram_steps, j, tile_rows):
            nc.sync.dma_start(out=dram_steps[j * SUBS : (j + 1) * SUBS].rearrange("r p h -> p r h"), in_=tile_rows)

        def new_c(j):
            hc = late.tile([P, 2, SUBS, H], F32)
            fc_ig = fc_ig_tiles[j]
            nc.vector.tensor_tensor(out=hc[:, 1], in0=fc_ig[:, :, 0:H], in1=fc_ig[:, :, H : 2 * H], op=ADD)
            store(hc_steps[1], j, hc[:, 1])
            hc_tiles[j] = hc

        def tanh_of_c(j):
            tanh_c = work.tile([P, SUBS, H], F32)
            nc.scalar.activation(out=tanh_c[:], in_=hc_tiles[j][:, 1], func=TANH)
            tanh_c_tiles[j] = tanh_c

        def new_h_and_store(j):
            hc = hc_tiles[j]
            o_gate = act_tiles[j][:, :, 2 * H : 3 * H]
            nc.vector.tensor_tensor(out=hc[:, 0], in0=o_gate, in1=tanh_c_tiles[j][:], op=MULT)
            store(hc_steps[0], j, hc[:, 0])
            store(out_0, j, hc[:, 0])

        def run(stage, j):
            if 0 <= j < ROUNDS:
                stage(j)

        def step(i):
            run(tanh_of_c, i - 2)
            run(copy_x, i + 2)
            run(gate_matmuls, i + 1)
            run(add_state_term, i)
            run(gate_functions, i)
            run(gate_products, i - 1)
            run(quantise_x, i + 2)
            run(new_c, i - 1)
            run(new_h_and_store, i - 2)
            run(transpose_x, i + 3)
            run(load_x, i + 3 + X_BUFS)

        for i in range(-3, PINNED_FROM):
            step(i)
        with tc.manual_schedule():
            for i in range(PINNED_FROM, ROUNDS + 2):
                step(i)
